import numpy as np
import ml_dtypes


def mxq(x, axis, fmt="e4m3"):
    dtype, down = {"e4m3": (ml_dtypes.float8_e4m3fn, 7), "e5m2": (ml_dtypes.float8_e5m2, 14)}[fmt]
    v = np.moveaxis(np.asarray(x, np.float32).astype(ml_dtypes.bfloat16).astype(np.float64), axis, -1)
    blocks = v.reshape(v.shape[:-1] + (-1, 32))
    amax = np.abs(blocks).max(-1, keepdims=True)
    byte = np.maximum(np.where(amax > 0, np.frexp(amax)[1] - 1 + 127, 0) - down, 1)
    scale = np.exp2(byte - 127.0)
    codes = (blocks / scale).astype(np.float32).astype(dtype).astype(np.float64)
    return np.moveaxis((codes * scale).reshape(v.shape), -1, axis)


WIDE = False


def mx_kscale(k):
    if not WIDE:
        return np.ones(k)
    levels = np.array([10, -10, 5, -5, 0])
    a = np.random.permutation(np.resize(levels, k // 512 * 4)).reshape(k // 512, 4)
    idx = np.arange(k)
    return np.exp2(a[idx // 512, idx % 128 // 32])


BF16 = ml_dtypes.bfloat16


def bf(x):
    return np.asarray(x, np.float32).astype(BF16)


def f64(x):
    return np.asarray(x).astype(np.float64)


B, T, C, E, DV, R, G, BLK = 4, 1024, 512, 1024, 1024, 16, 16, 512
BASE = 1e4


def rope(x):
    inv_freq = 1.0 / (BASE ** (f64(np.arange(0, R, 2)) / R))
    ang = f64(np.arange(T))[:, None] * inv_freq[None, :]
    ang = np.repeat(ang, 2, axis=-1)
    cos, sin = np.cos(ang), np.sin(ang)
    xl, xr = x[..., :R], x[..., R:]
    p = xl.reshape(xl.shape[:-1] + (R // 2, 2))
    rot = np.stack((-p[..., 1], p[..., 0]), axis=-1).reshape(xl.shape)
    return np.concatenate([xl * cos + rot * sin, xr], axis=-1)


def setup_inputs():
    s = mx_kscale(C)
    return {"Q_in": bf(np.random.standard_normal((B, T, C)) * s),
            "W_Q": bf(np.random.standard_normal((C, E)) * 0.25 / np.sqrt(C) / s[:, None]),
            "W_K": bf(np.random.standard_normal((C, E)) * 0.25 / np.sqrt(C) / s[:, None])}


def reference(Q_in, W_Q, W_K):
    xq = mxq(f64(Q_in), 2, "e4m3")
    q = rope(xq @ mxq(f64(W_Q), 0, "e4m3"))
    k = rope(xq @ mxq(f64(W_K), 0, "e4m3"))
    return q, k

@@ -1,0 +1,205 @@
+import math
+from contextlib import ExitStack
+
+import concourse.mybir as mybir
+from concourse.masks import make_identity
+
+F32 = mybir.dt.float32
+BF16 = mybir.dt.bfloat16
+I32 = mybir.dt.int32
+U32 = mybir.dt.uint32
+U8 = mybir.dt.uint8
+FP8X4 = mybir.dt.float8_e4m3fn_x4
+ALU = mybir.AluOpType
+ACT = mybir.ActivationFunctionType
+
+P = 128
+PACK = 4
+BATCH, SEQ, K, CH = 4, 1024, 512, 1024
+ROPE_CH = 16
+PAIRS = ROPE_CH // 2
+ROPE_BASE = 1e4
+TOK = SEQ // P
+TOK_STORE = 4
+STORES = TOK // TOK_STORE
+N_TILE = 512
+N_TILES = CH // N_TILE
+HALF_WORDS = K // 4
+
+FLOPS = 2 * BATCH * SEQ * K * 2 * CH
+
+TWO_PI = 2.0 * math.pi
+TURN_GRID = 2.0 ** 15
+ROUND_MAGIC = 1.5 * 2.0 ** 23
+
+
+def build_rotations(nc, consts):
+    shape = [P, 2, TOK, PAIRS, 2]
+
+    def flat(t):
+        return t[:].rearrange("p o j i e -> p (o j i e)")
+
+    position_int = consts.tile([P, TOK], I32)
+    nc.gpsimd.iota(position_int[:], pattern=[[1, TOK]], base=0, channel_multiplier=TOK)
+    position = consts.tile([P, TOK], F32)
+    nc.vector.tensor_copy(out=position[:], in_=position_int[:])
+    position_oje = position[:].unsqueeze(1).unsqueeze(3).to_broadcast([P, 2, TOK, 2])
+
+    coarse = consts.tile(shape, F32)
+    fine = consts.tile(shape, F32)
+    for i in range(PAIRS):
+        turns = ROPE_BASE ** (-2.0 * i / ROPE_CH) / TWO_PI
+        turns_coarse = round(turns * TURN_GRID) / TURN_GRID
+        nc.vector.tensor_scalar_mul(out=coarse[:, :, :, i, :], in0=position_oje, scalar1=turns_coarse)
+        nc.vector.tensor_scalar_mul(out=fine[:, :, :, i, :], in0=position_oje, scalar1=turns - turns_coarse)
+    for o in range(2):
+        nc.vector.tensor_scalar_add(out=coarse[:, o, :, :, o], in0=coarse[:, o, :, :, o], scalar1=0.25)
+
+    nearest = consts.tile(shape, F32)
+    nc.vector.tensor_add(out=flat(nearest), in0=flat(coarse), in1=flat(fine))
+    nc.vector.tensor_scalar(
+        out=flat(nearest), in0=flat(nearest), scalar1=ROUND_MAGIC, scalar2=ROUND_MAGIC, op0=ALU.add, op1=ALU.subtract
+    )
+    nc.vector.tensor_sub(out=flat(coarse), in0=flat(coarse), in1=flat(nearest))
+    nc.vector.tensor_add(out=flat(fine), in0=flat(coarse), in1=flat(fine))
+
+    rot = consts.tile(shape, F32)
+    nc.scalar.activation(out=flat(rot), in_=flat(fine), func=ACT.Sin, scale=TWO_PI)
+    nc.vector.tensor_scalar_mul(out=rot[:, 0, :, :, 1], in0=rot[:, 0, :, :, 1], scalar1=-1.0)
+    return rot
+
+
+def copy_by_parity(nc, n, out, in_):
+    if n % 2 == 0:
+        nc.vector.tensor_copy(out=out, in_=in_)
+    else:
+        nc.scalar.copy(out=out, in_=in_)
+
+
+def load_weight(nc, weights, w, label):
+    raw = weights.tile([P, PACK, CH], BF16, name="raw_" + label)
+    nc.sync.dma_start(
+        out=raw[:].rearrange("p (u e) c -> p u e c", e=2),
+        in_=w.rearrange("(u p e) c -> p u e c", u=2, e=2),
+    )
+    return raw
+
+
+def quantise_weight(nc, weights, raw, label):
+    grouped = weights.tile([P, CH, PACK], BF16, name="grouped_" + label, align_bytes=64)
+    codes = weights.tile([P, CH], U32, name="codes_" + label, align_bytes=64)
+    scales = weights.tile([P, CH], U8, name="scales_" + label, align_bytes=64)
+    for n in range(N_TILES):
+        cols = slice(n * N_TILE, (n + 1) * N_TILE)
+        copy_by_parity(
+            nc,
+            n,
+            out=grouped[:, cols, :].rearrange("p (c i) t -> p c t i", i=4),
+            in_=raw[:, :, cols].rearrange("p t (c i) -> p c t i", i=4),
+        )
+    for n in range(N_TILES):
+        cols = slice(n * N_TILE, (n + 1) * N_TILE)
+        nc.vector.quantize_mx(
+            out=codes[:, cols].bitcast(FP8X4),
+            scales=scales[:, cols],
+            in_=grouped[:, cols, :].rearrange("p c t -> p (c t)"),
+        )
+    return codes, scales
+
+
+def quantise_tokens(nc, tokens, staging, psum_t, identity, rows, b):
+    codes = tokens.tile([P, TOK * P], U32, name="x_codes%d" % b, align_bytes=64)
+    scales = tokens.tile([P, TOK * P], U8, name="x_scales%d" % b, align_bytes=64)
+    for s in range(STORES):
+        grouped = staging.tile([P, TOK_STORE * P * PACK], BF16, align_bytes=64)
+        grouped_words = grouped[:].bitcast(F32).rearrange("p (j r u) -> p j r u", j=TOK_STORE, u=2)
+        for m in range(TOK_STORE // 2):
+            flipped = psum_t.tile([P, 2, 2, P], F32)
+            for jj in range(2):
+                words = rows[:, s * TOK_STORE + 2 * m + jj, :].bitcast(F32)
+                for u in range(2):
+                    nc.tensor.transpose(
+                        out=flipped[:, jj, u, :],
+                        in_=words[:, u * HALF_WORDS : (u + 1) * HALF_WORDS],
+                        identity=identity[:],
+                    )
+            nc.scalar.copy(
+                out=grouped_words[:, 2 * m : 2 * m + 2, :, :],
+                in_=flipped[:].rearrange("p j u r -> p j r u"),
+            )
+        cols = slice(s * TOK_STORE * P, (s + 1) * TOK_STORE * P)
+        nc.vector.quantize_mx(out=codes[:, cols].bitcast(FP8X4), scales=scales[:, cols], in_=grouped[:])
+    return codes, scales
+
+
+def project(nc, stage_pool, small, psum_acc, x_mx, w_mx, rot, out_b):
+    x_codes, x_scales = x_mx
+    w_codes, w_scales = w_mx
+    out_pjc = out_b.rearrange("(p j) c -> p j c", j=TOK)
+    for s in range(STORES):
+        stage = stage_pool.tile([P, TOK_STORE, CH], F32)
+        for jj in range(TOK_STORE):
+            toks = slice((s * TOK_STORE + jj) * P, (s * TOK_STORE + jj + 1) * P)
+            for n in range(N_TILES):
+                cols = slice(n * N_TILE, (n + 1) * N_TILE)
+                acc = psum_acc.tile([P, N_TILE], F32)
+                nc.tensor.matmul_mx(
+                    out=acc[:],
+                    lhsT=x_codes[:, toks].bitcast(FP8X4),
+                    lhsT_scale=x_scales[:, toks],
+                    rhs=w_codes[:, cols].bitcast(FP8X4),
+                    rhs_scale=w_scales[:, cols],
+                    start=True,
+                    stop=True,
+                )
+                copy_by_parity(nc, n, out=stage[:, jj, cols], in_=acc[:])
+
+        x = stage[:, :, 0:ROPE_CH]
+        products = small.tile([P, 2, TOK_STORE, PAIRS, 2], F32)
+        nc.vector.tensor_tensor(
+            out=products[:].rearrange("p o j i e -> p o j (i e)"),
+            in0=x.unsqueeze(1).to_broadcast([P, 2, TOK_STORE, ROPE_CH]),
+            in1=rot[:, :, s * TOK_STORE : (s + 1) * TOK_STORE, :, :].rearrange("p o j i e -> p o j (i e)"),
+            op=ALU.mult,
+        )
+        nc.vector.tensor_tensor(
+            out=x.rearrange("p j (i o) -> p o j i", o=2),
+            in0=products[:, :, :, :, 0],
+            in1=products[:, :, :, :, 1],
+            op=ALU.add,
+        )
+        nc.sync.dma_start(out=out_pjc[:, s * TOK_STORE : (s + 1) * TOK_STORE, :], in_=stage[:])
+
+
+def tile_wqkv_pa_t_kernel(tc, Q_in, W_Q, W_K, out_0, out_1):
+    nc = tc.nc
+    with ExitStack() as ctx:
+        consts = ctx.enter_context(tc.tile_pool(name="consts", bufs=1))
+        weights = ctx.enter_context(tc.tile_pool(name="weights", bufs=1))
+        tokens = ctx.enter_context(tc.tile_pool(name="tokens", bufs=1))
+        staging = ctx.enter_context(tc.tile_pool(name="staging", bufs=2))
+        small = ctx.enter_context(tc.tile_pool(name="small", bufs=2))
+        stage_pool = ctx.enter_context(tc.tile_pool(name="stage", bufs=6))
+        psum_t = ctx.enter_context(tc.psum_pool(name="psum_t", bufs=2))
+        psum_acc = ctx.enter_context(tc.psum_pool(name="psum_acc", bufs=6))
+
+        rows = [tokens.tile([P, TOK, K], BF16, name="rows%d" % b) for b in range(BATCH)]
+        raw_q = load_weight(nc, weights, W_Q, "q")
+        nc.sync.dma_start(out=rows[0][:], in_=Q_in[0].rearrange("(p j) k -> p j k", j=TOK))
+        raw_k = load_weight(nc, weights, W_K, "k")
+        for b in range(1, BATCH):
+            nc.sync.dma_start(out=rows[b][:], in_=Q_in[b].rearrange("(p j) k -> p j k", j=TOK))
+
+        identity = consts.tile([P, P], F32)
+        make_identity(nc, identity[:])
+        rot = build_rotations(nc, consts)
+
+        wq_mx = quantise_weight(nc, weights, raw_q, "q")
+        x_mx = [quantise_tokens(nc, tokens, staging, psum_t, identity, rows[0], 0)]
+        for b in range(BATCH):
+            project(nc, stage_pool, small, psum_acc, x_mx[b], wq_mx, rot, out_0[b])
+            if b == 0:
+                wk_mx = quantise_weight(nc, weights, raw_k, "k")
+            if b + 1 < BATCH:
+                x_mx.append(quantise_tokens(nc, tokens, staging, psum_t, identity, rows[b + 1], b + 1))
+            project(nc, stage_pool, small, psum_acc, x_mx[b], wk_mx, rot, out_1[b])

@@ -34,38 +34,38 @@ ROUND_MAGIC = 1.5 * 2.0 ** 23
 
 
 def build_rotations(nc, consts):
-    shape = [P, 2, TOK, PAIRS, 2]
-
-    def flat(t):
-        return t[:].rearrange("p o j i e -> p (o j i e)")
-
     position_int = consts.tile([P, TOK], I32)
     nc.gpsimd.iota(position_int[:], pattern=[[1, TOK]], base=0, channel_multiplier=TOK)
     position = consts.tile([P, TOK], F32)
     nc.vector.tensor_copy(out=position[:], in_=position_int[:])
-    position_oje = position[:].unsqueeze(1).unsqueeze(3).to_broadcast([P, 2, TOK, 2])
 
-    coarse = consts.tile(shape, F32)
-    fine = consts.tile(shape, F32)
+    coarse = consts.tile([P, 2, TOK, PAIRS], F32)
+    fine = consts.tile([P, TOK, PAIRS], F32)
     for i in range(PAIRS):
         turns = ROPE_BASE ** (-2.0 * i / ROPE_CH) / TWO_PI
         turns_coarse = round(turns * TURN_GRID) / TURN_GRID
-        nc.vector.tensor_scalar_mul(out=coarse[:, :, :, i, :], in0=position_oje, scalar1=turns_coarse)
-        nc.vector.tensor_scalar_mul(out=fine[:, :, :, i, :], in0=position_oje, scalar1=turns - turns_coarse)
-    for o in range(2):
-        nc.vector.tensor_scalar_add(out=coarse[:, o, :, :, o], in0=coarse[:, o, :, :, o], scalar1=0.25)
+        nc.vector.tensor_scalar_mul(out=coarse[:, 0, :, i], in0=position[:], scalar1=turns_coarse)
+        nc.vector.tensor_scalar_mul(out=fine[:, :, i], in0=position[:], scalar1=turns - turns_coarse)
+    nc.vector.tensor_scalar_add(out=coarse[:, 1, :, :], in0=coarse[:, 0, :, :], scalar1=0.25)
 
-    nearest = consts.tile(shape, F32)
-    nc.vector.tensor_add(out=flat(nearest), in0=flat(coarse), in1=flat(fine))
+    fine_twice = fine[:].unsqueeze(1).to_broadcast([P, 2, TOK, PAIRS])
+    whole = consts.tile([P, 2, TOK, PAIRS], F32)
+    nc.vector.tensor_tensor(out=whole[:], in0=coarse[:], in1=fine_twice, op=ALU.add)
     nc.vector.tensor_scalar(
-        out=flat(nearest), in0=flat(nearest), scalar1=ROUND_MAGIC, scalar2=ROUND_MAGIC, op0=ALU.add, op1=ALU.subtract
+        out=whole[:], in0=whole[:], scalar1=ROUND_MAGIC, scalar2=ROUND_MAGIC, op0=ALU.add, op1=ALU.subtract
     )
-    nc.vector.tensor_sub(out=flat(coarse), in0=flat(coarse), in1=flat(nearest))
-    nc.vector.tensor_add(out=flat(fine), in0=flat(coarse), in1=flat(fine))
+    nc.vector.tensor_tensor(out=coarse[:], in0=coarse[:], in1=whole[:], op=ALU.subtract)
+    reduced = consts.tile([P, 2, TOK, PAIRS], F32)
+    nc.vector.tensor_tensor(out=reduced[:], in0=coarse[:], in1=fine_twice, op=ALU.add)
 
-    rot = consts.tile(shape, F32)
-    nc.scalar.activation(out=flat(rot), in_=flat(fine), func=ACT.Sin, scale=TWO_PI)
-    nc.vector.tensor_scalar_mul(out=rot[:, 0, :, :, 1], in0=rot[:, 0, :, :, 1], scalar1=-1.0)
+    rot = consts.tile([P, 2, TOK, PAIRS, 2], F32)
+    for o in range(2):
+        for e in range(2):
+            quarter_ahead = 1 if o == e else 0
+            sign = -1.0 if o < e else 1.0
+            nc.scalar.activation(
+                out=rot[:, o, :, :, e], in_=reduced[:, quarter_ahead, :, :], func=ACT.Sin, scale=sign * TWO_PI
+            )
     return rot
 
 
@@ -107,76 +107,72 @@ def quantise_weight(nc, weights, raw, label):
     return codes, scales
 
 
-def quantise_tokens(nc, tokens, staging, psum_t, identity, rows, b):
-    codes = tokens.tile([P, TOK * P], U32, name="x_codes%d" % b, align_bytes=64)
-    scales = tokens.tile([P, TOK * P], U8, name="x_scales%d" % b, align_bytes=64)
-    for s in range(STORES):
-        grouped = staging.tile([P, TOK_STORE * P * PACK], BF16, align_bytes=64)
-        grouped_words = grouped[:].bitcast(F32).rearrange("p (j r u) -> p j r u", j=TOK_STORE, u=2)
-        for m in range(TOK_STORE // 2):
-            flipped = psum_t.tile([P, 2, 2, P], F32)
-            for jj in range(2):
-                words = rows[:, s * TOK_STORE + 2 * m + jj, :].bitcast(F32)
-                for u in range(2):
-                    nc.tensor.transpose(
-                        out=flipped[:, jj, u, :],
-                        in_=words[:, u * HALF_WORDS : (u + 1) * HALF_WORDS],
-                        identity=identity[:],
-                    )
-            nc.scalar.copy(
-                out=grouped_words[:, 2 * m : 2 * m + 2, :, :],
-                in_=flipped[:].rearrange("p j u r -> p j r u"),
-            )
-        cols = slice(s * TOK_STORE * P, (s + 1) * TOK_STORE * P)
-        nc.vector.quantize_mx(out=codes[:, cols].bitcast(FP8X4), scales=scales[:, cols], in_=grouped[:])
-    return codes, scales
+def quantise_tokens(nc, staging, psum_t, identity, rows, codes, scales, s):
+    grouped = staging.tile([P, TOK_STORE * P * PACK], BF16, align_bytes=64)
+    grouped_words = grouped[:].bitcast(F32).rearrange("p (j r u) -> p j r u", j=TOK_STORE, u=2)
+    for m in range(TOK_STORE // 2):
+        flipped = psum_t.tile([P, 2, 2, P], F32)
+        for jj in range(2):
+            words = rows[:, s * TOK_STORE + 2 * m + jj, :].bitcast(F32)
+            for u in range(2):
+                nc.tensor.transpose(
+                    out=flipped[:, jj, u, :],
+                    in_=words[:, u * HALF_WORDS : (u + 1) * HALF_WORDS],
+                    identity=identity[:],
+                )
+        nc.scalar.copy(
+            out=grouped_words[:, 2 * m : 2 * m + 2, :, :],
+            in_=flipped[:].rearrange("p j u r -> p j r u"),
+        )
+    cols = slice(s * TOK_STORE * P, (s + 1) * TOK_STORE * P)
+    nc.vector.quantize_mx(out=codes[:, cols].bitcast(FP8X4), scales=scales[:, cols], in_=grouped[:])
 
 
-def project(nc, stage_pool, small, psum_acc, x_mx, w_mx, rot, out_b):
-    x_codes, x_scales = x_mx
+def project(nc, stage_pool, small, psum_acc, x_codes, x_scales, w_mx, rot, out_b, s):
     w_codes, w_scales = w_mx
-    out_pjc = out_b.rearrange("(p j) c -> p j c", j=TOK)
-    for s in range(STORES):
-        stage = stage_pool.tile([P, TOK_STORE, CH], F32)
+    stage = stage_pool.tile([P, TOK_STORE, CH], F32)
+    for n in range(N_TILES):
+        cols = slice(n * N_TILE, (n + 1) * N_TILE)
         for jj in range(TOK_STORE):
             toks = slice((s * TOK_STORE + jj) * P, (s * TOK_STORE + jj + 1) * P)
-            for n in range(N_TILES):
-                cols = slice(n * N_TILE, (n + 1) * N_TILE)
-                acc = psum_acc.tile([P, N_TILE], F32)
-                nc.tensor.matmul_mx(
-                    out=acc[:],
-                    lhsT=x_codes[:, toks].bitcast(FP8X4),
-                    lhsT_scale=x_scales[:, toks],
-                    rhs=w_codes[:, cols].bitcast(FP8X4),
-                    rhs_scale=w_scales[:, cols],
-                    start=True,
-                    stop=True,
-                )
-                copy_by_parity(nc, n, out=stage[:, jj, cols], in_=acc[:])
+            acc = psum_acc.tile([P, N_TILE], F32)
+            nc.tensor.matmul_mx(
+                out=acc[:],
+                lhsT=x_codes[:, toks].bitcast(FP8X4),
+                lhsT_scale=x_scales[:, toks],
+                rhs=w_codes[:, cols].bitcast(FP8X4),
+                rhs_scale=w_scales[:, cols],
+                start=True,
+                stop=True,
+            )
+            copy_by_parity(nc, n, out=stage[:, jj, cols], in_=acc[:])
 
-        x = stage[:, :, 0:ROPE_CH]
-        products = small.tile([P, 2, TOK_STORE, PAIRS, 2], F32)
-        nc.vector.tensor_tensor(
-            out=products[:].rearrange("p o j i e -> p o j (i e)"),
-            in0=x.unsqueeze(1).to_broadcast([P, 2, TOK_STORE, ROPE_CH]),
-            in1=rot[:, :, s * TOK_STORE : (s + 1) * TOK_STORE, :, :].rearrange("p o j i e -> p o j (i e)"),
-            op=ALU.mult,
-        )
-        nc.vector.tensor_tensor(
-            out=x.rearrange("p j (i o) -> p o j i", o=2),
-            in0=products[:, :, :, :, 0],
-            in1=products[:, :, :, :, 1],
-            op=ALU.add,
-        )
-        nc.sync.dma_start(out=out_pjc[:, s * TOK_STORE : (s + 1) * TOK_STORE, :], in_=stage[:])
+    x = stage[:, :, 0:ROPE_CH]
+    products = small.tile([P, 2, TOK_STORE, PAIRS, 2], F32)
+    nc.vector.tensor_tensor(
+        out=products[:].rearrange("p o j i e -> p o j (i e)"),
+        in0=x.unsqueeze(1).to_broadcast([P, 2, TOK_STORE, ROPE_CH]),
+        in1=rot[:, :, s * TOK_STORE : (s + 1) * TOK_STORE, :, :].rearrange("p o j i e -> p o j (i e)"),
+        op=ALU.mult,
+    )
+    nc.vector.tensor_tensor(
+        out=x.rearrange("p j (i o) -> p o j i", o=2),
+        in0=products[:, :, :, :, 0],
+        in1=products[:, :, :, :, 1],
+        op=ALU.add,
+    )
+    out_pjc = out_b.rearrange("(p j) c -> p j c", j=TOK)
+    nc.sync.dma_start(out=out_pjc[:, s * TOK_STORE : (s + 1) * TOK_STORE, :], in_=stage[:])
 
 
 def tile_wqkv_pa_t_kernel(tc, Q_in, W_Q, W_K, out_0, out_1):
     nc = tc.nc
     with ExitStack() as ctx:
+        ctx.enter_context(tc.manual_schedule())
         consts = ctx.enter_context(tc.tile_pool(name="consts", bufs=1))
         weights = ctx.enter_context(tc.tile_pool(name="weights", bufs=1))
         tokens = ctx.enter_context(tc.tile_pool(name="tokens", bufs=1))
+        packed = ctx.enter_context(tc.tile_pool(name="packed", bufs=2))
         staging = ctx.enter_context(tc.tile_pool(name="staging", bufs=2))
         small = ctx.enter_context(tc.tile_pool(name="small", bufs=2))
         stage_pool = ctx.enter_context(tc.tile_pool(name="stage", bufs=6))
@@ -184,22 +180,27 @@ def tile_wqkv_pa_t_kernel(tc, Q_in, W_Q, W_K, out_0, out_1):
         psum_acc = ctx.enter_context(tc.psum_pool(name="psum_acc", bufs=6))
 
         rows = [tokens.tile([P, TOK, K], BF16, name="rows%d" % b) for b in range(BATCH)]
+        tokens_pjk = [Q_in[b].rearrange("(p j) k -> p j k", j=TOK) for b in range(BATCH)]
+        nc.sync.dma_start(out=rows[0][:, 0:TOK_STORE, :], in_=tokens_pjk[0][:, 0:TOK_STORE, :])
         raw_q = load_weight(nc, weights, W_Q, "q")
-        nc.sync.dma_start(out=rows[0][:], in_=Q_in[0].rearrange("(p j) k -> p j k", j=TOK))
+        nc.sync.dma_start(out=rows[0][:, TOK_STORE:TOK, :], in_=tokens_pjk[0][:, TOK_STORE:TOK, :])
         raw_k = load_weight(nc, weights, W_K, "k")
         for b in range(1, BATCH):
-            nc.sync.dma_start(out=rows[b][:], in_=Q_in[b].rearrange("(p j) k -> p j k", j=TOK))
+            nc.sync.dma_start(out=rows[b][:], in_=tokens_pjk[b])
 
+        rot = build_rotations(nc, consts)
         identity = consts.tile([P, P], F32)
         make_identity(nc, identity[:])
-        rot = build_rotations(nc, consts)
 
-        wq_mx = quantise_weight(nc, weights, raw_q, "q")
-        x_mx = [quantise_tokens(nc, tokens, staging, psum_t, identity, rows[0], 0)]
         for b in range(BATCH):
-            project(nc, stage_pool, small, psum_acc, x_mx[b], wq_mx, rot, out_0[b])
+            x_codes = packed.tile([P, TOK * P], U32, align_bytes=64)
+            x_scales = packed.tile([P, TOK * P], U8, align_bytes=64)
+            for s in range(STORES):
+                quantise_tokens(nc, staging, psum_t, identity, rows[b], x_codes, x_scales, s)
+                if b == 0 and s == 0:
+                    wq_mx = quantise_weight(nc, weights, raw_q, "q")
+                project(nc, stage_pool, small, psum_acc, x_codes, x_scales, wq_mx, rot, out_0[b], s)
             if b == 0:
                 wk_mx = quantise_weight(nc, weights, raw_k, "k")
-            if b + 1 < BATCH:
-                x_mx.append(quantise_tokens(nc, tokens, staging, psum_t, identity, rows[b + 1], b + 1))
-            project(nc, stage_pool, small, psum_acc, x_mx[b], wk_mx, rot, out_1[b])
+            for s in range(STORES):
+                project(nc, stage_pool, small, psum_acc, x_codes, x_scales, wk_mx, rot, out_1[b], s)

@@ -107,34 +107,44 @@ def quantise_weight(nc, weights, raw, label):
     return codes, scales
 
 
-def quantise_tokens(nc, staging, psum_t, identity, rows, codes, scales, s):
-    grouped = staging.tile([P, TOK_STORE * P * PACK], BF16, align_bytes=64)
-    grouped_words = grouped[:].bitcast(F32).rearrange("p (j r u) -> p j r u", j=TOK_STORE, u=2)
+def transpose_tokens(nc, psum_t, identity, rows):
+    banks = []
     for m in range(TOK_STORE // 2):
         flipped = psum_t.tile([P, 2, 2, P], F32)
         for jj in range(2):
-            words = rows[:, s * TOK_STORE + 2 * m + jj, :].bitcast(F32)
+            words = rows[:, 2 * m + jj, :].bitcast(F32)
             for u in range(2):
                 nc.tensor.transpose(
                     out=flipped[:, jj, u, :],
                     in_=words[:, u * HALF_WORDS : (u + 1) * HALF_WORDS],
                     identity=identity[:],
                 )
+        banks.append(flipped)
+    return banks
+
+
+def quantise_tokens(nc, staging, packed, banks):
+    grouped = staging.tile([P, TOK_STORE * P * PACK], BF16, align_bytes=64)
+    grouped_words = grouped[:].bitcast(F32).rearrange("p (j r u) -> p j r u", j=TOK_STORE, u=2)
+    for m in range(TOK_STORE // 2):
         nc.scalar.copy(
             out=grouped_words[:, 2 * m : 2 * m + 2, :, :],
-            in_=flipped[:].rearrange("p j u r -> p j r u"),
+            in_=banks[m][:].rearrange("p j u r -> p j r u"),
         )
-    cols = slice(s * TOK_STORE * P, (s + 1) * TOK_STORE * P)
-    nc.vector.quantize_mx(out=codes[:, cols].bitcast(FP8X4), scales=scales[:, cols], in_=grouped[:])
+    x_codes = packed.tile([P, TOK_STORE * P], U32, align_bytes=64)
+    x_scales = packed.tile([P, TOK_STORE * P], U8, align_bytes=64)
+    nc.vector.quantize_mx(out=x_codes[:].bitcast(FP8X4), scales=x_scales[:], in_=grouped[:])
+    return x_codes, x_scales
 
 
-def project(nc, stage_pool, small, psum_acc, x_codes, x_scales, w_mx, rot, out_b, s):
+def project(nc, stage_pool, small, psum_acc, x_mx, w_mx, rot, out_pjc):
+    x_codes, x_scales = x_mx
     w_codes, w_scales = w_mx
     stage = stage_pool.tile([P, TOK_STORE, CH], F32)
-    for n in range(N_TILES):
-        cols = slice(n * N_TILE, (n + 1) * N_TILE)
-        for jj in range(TOK_STORE):
-            toks = slice((s * TOK_STORE + jj) * P, (s * TOK_STORE + jj + 1) * P)
+    for j in range(TOK_STORE):
+        toks = slice(j * P, (j + 1) * P)
+        for n in range(N_TILES):
+            cols = slice(n * N_TILE, (n + 1) * N_TILE)
             acc = psum_acc.tile([P, N_TILE], F32)
             nc.tensor.matmul_mx(
                 out=acc[:],
@@ -145,14 +155,14 @@ def project(nc, stage_pool, small, psum_acc, x_codes, x_scales, w_mx, rot, out_b
                 start=True,
                 stop=True,
             )
-            copy_by_parity(nc, n, out=stage[:, jj, cols], in_=acc[:])
+            copy_by_parity(nc, n, out=stage[:, j, cols], in_=acc[:])
 
     x = stage[:, :, 0:ROPE_CH]
     products = small.tile([P, 2, TOK_STORE, PAIRS, 2], F32)
     nc.vector.tensor_tensor(
         out=products[:].rearrange("p o j i e -> p o j (i e)"),
         in0=x.unsqueeze(1).to_broadcast([P, 2, TOK_STORE, ROPE_CH]),
-        in1=rot[:, :, s * TOK_STORE : (s + 1) * TOK_STORE, :, :].rearrange("p o j i e -> p o j (i e)"),
+        in1=rot.rearrange("p o j i e -> p o j (i e)"),
         op=ALU.mult,
     )
     nc.vector.tensor_tensor(
@@ -161,8 +171,7 @@ def project(nc, stage_pool, small, psum_acc, x_codes, x_scales, w_mx, rot, out_b
         in1=products[:, :, :, :, 1],
         op=ALU.add,
     )
-    out_pjc = out_b.rearrange("(p j) c -> p j c", j=TOK)
-    nc.sync.dma_start(out=out_pjc[:, s * TOK_STORE : (s + 1) * TOK_STORE, :], in_=stage[:])
+    nc.sync.dma_start(out=out_pjc, in_=stage[:])
 
 
 def tile_wqkv_pa_t_kernel(tc, Q_in, W_Q, W_K, out_0, out_1):
@@ -180,27 +189,37 @@ def tile_wqkv_pa_t_kernel(tc, Q_in, W_Q, W_K, out_0, out_1):
         psum_acc = ctx.enter_context(tc.psum_pool(name="psum_acc", bufs=6))
 
         rows = [tokens.tile([P, TOK, K], BF16, name="rows%d" % b) for b in range(BATCH)]
-        tokens_pjk = [Q_in[b].rearrange("(p j) k -> p j k", j=TOK) for b in range(BATCH)]
-        nc.sync.dma_start(out=rows[0][:, 0:TOK_STORE, :], in_=tokens_pjk[0][:, 0:TOK_STORE, :])
-        raw_q = load_weight(nc, weights, W_Q, "q")
-        nc.sync.dma_start(out=rows[0][:, TOK_STORE:TOK, :], in_=tokens_pjk[0][:, TOK_STORE:TOK, :])
-        raw_k = load_weight(nc, weights, W_K, "k")
-        for b in range(1, BATCH):
-            nc.sync.dma_start(out=rows[b][:], in_=tokens_pjk[b])
-
+        group_rows, group_in, group_q, group_k, group_rot = [], [], [], [], []
         rot = build_rotations(nc, consts)
+        for b in range(BATCH):
+            for first in range(0, TOK, TOK_STORE):
+                js = slice(first, first + TOK_STORE)
+                group_rows.append(rows[b][:, js, :])
+                group_in.append(Q_in[b].rearrange("(p j) k -> p j k", j=TOK)[:, js, :])
+                group_q.append(out_0[b].rearrange("(p j) c -> p j c", j=TOK)[:, js, :])
+                group_k.append(out_1[b].rearrange("(p j) c -> p j c", j=TOK)[:, js, :])
+                group_rot.append(rot[:, :, js, :, :])
+        groups = len(group_rows)
+
+        nc.sync.dma_start(out=group_rows[0], in_=group_in[0])
+        raw_q = load_weight(nc, weights, W_Q, "q")
+        nc.sync.dma_start(out=group_rows[1], in_=group_in[1])
+        raw_k = load_weight(nc, weights, W_K, "k")
+        for g in range(2, groups):
+            nc.sync.dma_start(out=group_rows[g], in_=group_in[g])
+
         identity = consts.tile([P, P], F32)
         make_identity(nc, identity[:])
 
-        for b in range(BATCH):
-            x_codes = packed.tile([P, TOK * P], U32, align_bytes=64)
-            x_scales = packed.tile([P, TOK * P], U8, align_bytes=64)
-            for s in range(STORES):
-                quantise_tokens(nc, staging, psum_t, identity, rows[b], x_codes, x_scales, s)
-                if b == 0 and s == 0:
-                    wq_mx = quantise_weight(nc, weights, raw_q, "q")
-                project(nc, stage_pool, small, psum_acc, x_codes, x_scales, wq_mx, rot, out_0[b], s)
-            if b == 0:
+        x_next = quantise_tokens(nc, staging, packed, transpose_tokens(nc, psum_t, identity, group_rows[0]))
+        wq_mx = quantise_weight(nc, weights, raw_q, "q")
+        for g in range(groups):
+            x_mx = x_next
+            if g + 1 < groups:
+                banks = transpose_tokens(nc, psum_t, identity, group_rows[g + 1])
+            project(nc, stage_pool, small, psum_acc, x_mx, wq_mx, group_rot[g], group_q[g])
+            if g == 0:
                 wk_mx = quantise_weight(nc, weights, raw_k, "k")
-            for s in range(STORES):
-                project(nc, stage_pool, small, psum_acc, x_codes, x_scales, wk_mx, rot, out_1[b], s)
+            if g + 1 < groups:
+                x_next = quantise_tokens(nc, staging, packed, banks)
+            project(nc, stage_pool, small, psum_acc, x_mx, wk_mx, group_rot[g], group_k[g])

@@ -24,7 +24,6 @@ TOK_STORE = 4
 STORES = TOK // TOK_STORE
 N_TILE = 512
 N_TILES = CH // N_TILE
-HALF_WORDS = K // 4
 
 FLOPS = 2 * BATCH * SEQ * K * 2 * CH
 
@@ -78,10 +77,7 @@ def copy_by_parity(nc, n, out, in_):
 
 def load_weight(nc, weights, w, label):
     raw = weights.tile([P, PACK, CH], BF16, name="raw_" + label)
-    nc.sync.dma_start(
-        out=raw[:].rearrange("p (u e) c -> p u e c", e=2),
-        in_=w.rearrange("(u p e) c -> p u e c", u=2, e=2),
-    )
+    nc.sync.dma_start(out=raw[:], in_=w.rearrange("(p t) c -> p t c", t=PACK))
     return raw
 
 
@@ -112,13 +108,9 @@ def transpose_tokens(nc, psum_t, identity, rows):
     for m in range(TOK_STORE // 2):
         flipped = psum_t.tile([P, 2, 2, P], F32)
         for jj in range(2):
-            words = rows[:, 2 * m + jj, :].bitcast(F32)
+            words = rows[:, 2 * m + jj, :].bitcast(F32).rearrange("r (q u) -> r u q", u=2)
             for u in range(2):
-                nc.tensor.transpose(
-                    out=flipped[:, jj, u, :],
-                    in_=words[:, u * HALF_WORDS : (u + 1) * HALF_WORDS],
-                    identity=identity[:],
-                )
+                nc.tensor.transpose(out=flipped[:, jj, u, :], in_=words[:, u, :], identity=identity[:])
         banks.append(flipped)
     return banks
 

@@ -176,7 +176,7 @@ def tile_wqkv_pa_t_kernel(tc, Q_in, W_Q, W_K, out_0, out_1):
         packed = ctx.enter_context(tc.tile_pool(name="packed", bufs=2))
         staging = ctx.enter_context(tc.tile_pool(name="staging", bufs=2))
         small = ctx.enter_context(tc.tile_pool(name="small", bufs=2))
-        stage_pool = ctx.enter_context(tc.tile_pool(name="stage", bufs=6))
+        stage_pool = ctx.enter_context(tc.tile_pool(name="stage", bufs=8))
         psum_t = ctx.enter_context(tc.psum_pool(name="psum_t", bufs=2))
         psum_acc = ctx.enter_context(tc.psum_pool(name="psum_acc", bufs=6))
 

@@ -68,8 +68,8 @@ def build_rotations(nc, consts):
     return rot
 
 
-def copy_by_parity(nc, n, out, in_):
-    if n % 2 == 0:
+def copy_on(nc, on_vector, out, in_):
+    if on_vector:
         nc.vector.tensor_copy(out=out, in_=in_)
     else:
         nc.scalar.copy(out=out, in_=in_)
@@ -81,26 +81,30 @@ def load_weight(nc, weights, w, label):
     return raw
 
 
-def quantise_weight(nc, weights, raw, label):
+def weight_tiles(weights, label):
     grouped = weights.tile([P, CH, PACK], BF16, name="grouped_" + label, align_bytes=64)
     codes = weights.tile([P, CH], U32, name="codes_" + label, align_bytes=64)
     scales = weights.tile([P, CH], U8, name="scales_" + label, align_bytes=64)
-    for n in range(N_TILES):
-        cols = slice(n * N_TILE, (n + 1) * N_TILE)
-        copy_by_parity(
-            nc,
-            n,
-            out=grouped[:, cols, :].rearrange("p (c i) t -> p c t i", i=4),
-            in_=raw[:, :, cols].rearrange("p t (c i) -> p c t i", i=4),
-        )
-    for n in range(N_TILES):
-        cols = slice(n * N_TILE, (n + 1) * N_TILE)
-        nc.vector.quantize_mx(
-            out=codes[:, cols].bitcast(FP8X4),
-            scales=scales[:, cols],
-            in_=grouped[:, cols, :].rearrange("p c t -> p (c t)"),
-        )
-    return codes, scales
+    return grouped, codes, scales
+
+
+def interleave_weight(nc, on_vector, raw, tiles, cols):
+    grouped = tiles[0]
+    copy_on(
+        nc,
+        on_vector,
+        out=grouped[:, cols, :].rearrange("p (c i) t -> p c t i", i=4),
+        in_=raw[:, :, cols].rearrange("p t (c i) -> p c t i", i=4),
+    )
+
+
+def quantise_weight(nc, tiles, cols):
+    grouped, codes, scales = tiles
+    nc.vector.quantize_mx(
+        out=codes[:, cols].bitcast(FP8X4),
+        scales=scales[:, cols],
+        in_=grouped[:, cols, :].rearrange("p c t -> p (c t)"),
+    )
 
 
 def transpose_tokens(nc, psum_t, identity, rows):
@@ -129,32 +133,33 @@ def quantise_tokens(nc, staging, packed, banks):
     return x_codes, x_scales
 
 
-def project(nc, stage_pool, small, psum_acc, x_mx, w_mx, rot, out_pjc):
+def multiply(nc, psum_acc, stage, j, x_mx, w_tiles, on_vector):
     x_codes, x_scales = x_mx
-    w_codes, w_scales = w_mx
-    stage = stage_pool.tile([P, TOK_STORE, CH], F32)
-    for j in range(TOK_STORE):
-        toks = slice(j * P, (j + 1) * P)
-        for n in range(N_TILES):
-            cols = slice(n * N_TILE, (n + 1) * N_TILE)
-            acc = psum_acc.tile([P, N_TILE], F32)
-            nc.tensor.matmul_mx(
-                out=acc[:],
-                lhsT=x_codes[:, toks].bitcast(FP8X4),
-                lhsT_scale=x_scales[:, toks],
-                rhs=w_codes[:, cols].bitcast(FP8X4),
-                rhs_scale=w_scales[:, cols],
-                start=True,
-                stop=True,
-            )
-            copy_by_parity(nc, n, out=stage[:, j, cols], in_=acc[:])
+    w_codes, w_scales = w_tiles[1], w_tiles[2]
+    toks = slice(j * P, (j + 1) * P)
+    for n in range(N_TILES):
+        cols = slice(n * N_TILE, (n + 1) * N_TILE)
+        acc = psum_acc.tile([P, N_TILE], F32)
+        nc.tensor.matmul_mx(
+            out=acc[:],
+            lhsT=x_codes[:, toks].bitcast(FP8X4),
+            lhsT_scale=x_scales[:, toks],
+            rhs=w_codes[:, cols].bitcast(FP8X4),
+            rhs_scale=w_scales[:, cols],
+            start=True,
+            stop=True,
+        )
+        copy_on(nc, on_vector[n], out=stage[:, j, cols], in_=acc[:])
 
-    x = stage[:, :, 0:ROPE_CH]
-    products = small.tile([P, 2, TOK_STORE, PAIRS, 2], F32)
+
+def rotate_and_store(nc, small, stage, js, rot, out_pjc):
+    count = js.stop - js.start
+    x = stage[:, js, 0:ROPE_CH]
+    products = small.tile([P, 2, count, PAIRS, 2], F32)
     nc.vector.tensor_tensor(
         out=products[:].rearrange("p o j i e -> p o j (i e)"),
-        in0=x.unsqueeze(1).to_broadcast([P, 2, TOK_STORE, ROPE_CH]),
-        in1=rot.rearrange("p o j i e -> p o j (i e)"),
+        in0=x.unsqueeze(1).to_broadcast([P, 2, count, ROPE_CH]),
+        in1=rot[:, :, js, :, :].rearrange("p o j i e -> p o j (i e)"),
         op=ALU.mult,
     )
     nc.vector.tensor_tensor(
@@ -163,7 +168,15 @@ def project(nc, stage_pool, small, psum_acc, x_mx, w_mx, rot, out_pjc):
         in1=products[:, :, :, :, 1],
         op=ALU.add,
     )
-    nc.sync.dma_start(out=out_pjc, in_=stage[:])
+    nc.sync.dma_start(out=out_pjc[:, js, :], in_=stage[:, js, :])
+
+
+def project(nc, stage_pool, small, psum_acc, x_mx, w_tiles, rot, out_pjc, per_store):
+    stage = stage_pool.tile([P, TOK_STORE, CH], F32)
+    for first in range(0, TOK_STORE, per_store):
+        for j in range(first, first + per_store):
+            multiply(nc, psum_acc, stage, j, x_mx, w_tiles, (True, False))
+        rotate_and_store(nc, small, stage, slice(first, first + per_store), rot, out_pjc)
 
 
 def tile_wqkv_pa_t_kernel(tc, Q_in, W_Q, W_K, out_0, out_1):
@@ -195,23 +208,43 @@ def tile_wqkv_pa_t_kernel(tc, Q_in, W_Q, W_K, out_0, out_1):
 
         nc.sync.dma_start(out=group_rows[0], in_=group_in[0])
         raw_q = load_weight(nc, weights, W_Q, "q")
-        nc.sync.dma_start(out=group_rows[1], in_=group_in[1])
         raw_k = load_weight(nc, weights, W_K, "k")
-        for g in range(2, groups):
+        for g in range(1, groups):
             nc.sync.dma_start(out=group_rows[g], in_=group_in[g])
 
         identity = consts.tile([P, P], F32)
         make_identity(nc, identity[:])
 
-        x_next = quantise_tokens(nc, staging, packed, transpose_tokens(nc, psum_t, identity, group_rows[0]))
-        wq_mx = quantise_weight(nc, weights, raw_q, "q")
-        for g in range(groups):
+        halves = [slice(n * N_TILE, (n + 1) * N_TILE) for n in range(N_TILES)]
+        quarters = [slice(u * CH // 4, (u + 1) * CH // 4) for u in range(4)]
+
+        x_mx = quantise_tokens(nc, staging, packed, transpose_tokens(nc, psum_t, identity, group_rows[0]))
+        wq = weight_tiles(weights, "q")
+        interleave_weight(nc, True, raw_q, wq, halves[0])
+        interleave_weight(nc, False, raw_q, wq, halves[1])
+        quantise_weight(nc, wq, halves[0])
+        quantise_weight(nc, wq, halves[1])
+
+        wk = weight_tiles(weights, "k")
+        stage = stage_pool.tile([P, TOK_STORE, CH], F32)
+        interleave_weight(nc, True, raw_k, wk, quarters[0])
+        for j in range(TOK_STORE):
+            multiply(nc, psum_acc, stage, j, x_mx, wq, (False, False))
+            if j + 1 < 4:
+                interleave_weight(nc, True, raw_k, wk, quarters[j + 1])
+            else:
+                quantise_weight(nc, wk, halves[0])
+            rotate_and_store(nc, small, stage, slice(j, j + 1), group_rot[0], group_q[0])
+        quantise_weight(nc, wk, halves[1])
+
+        x_next = quantise_tokens(nc, staging, packed, transpose_tokens(nc, psum_t, identity, group_rows[1]))
+        project(nc, stage_pool, small, psum_acc, x_mx, wk, group_rot[0], group_k[0], 1)
+
+        for g in range(1, groups):
             x_mx = x_next
             if g + 1 < groups:
                 banks = transpose_tokens(nc, psum_t, identity, group_rows[g + 1])
-            project(nc, stage_pool, small, psum_acc, x_mx, wq_mx, group_rot[g], group_q[g])
-            if g == 0:
-                wk_mx = quantise_weight(nc, weights, raw_k, "k")
+            project(nc, stage_pool, small, psum_acc, x_mx, wq, group_rot[g], group_q[g], TOK_STORE)
             if g + 1 < groups:
                 x_next = quantise_tokens(nc, staging, packed, banks)
-            project(nc, stage_pool, small, psum_acc, x_mx, wk_mx, group_rot[g], group_k[g])
+            project(nc, stage_pool, small, psum_acc, x_mx, wk, group_rot[g], group_k[g], TOK_STORE)

@@ -119,7 +119,7 @@ def transpose_tokens(nc, psum_t, identity, rows):
     return banks
 
 
-def quantise_tokens(nc, staging, packed, banks):
+def copy_tokens(nc, staging, banks):
     grouped = staging.tile([P, TOK_STORE * P * PACK], BF16, align_bytes=64)
     grouped_words = grouped[:].bitcast(F32).rearrange("p (j r u) -> p j r u", j=TOK_STORE, u=2)
     for m in range(TOK_STORE // 2):
@@ -127,6 +127,10 @@ def quantise_tokens(nc, staging, packed, banks):
             out=grouped_words[:, 2 * m : 2 * m + 2, :, :],
             in_=banks[m][:].rearrange("p j u r -> p j r u"),
         )
+    return grouped
+
+
+def quantise_tokens(nc, packed, grouped):
     x_codes = packed.tile([P, TOK_STORE * P], U32, align_bytes=64)
     x_scales = packed.tile([P, TOK_STORE * P], U8, align_bytes=64)
     nc.vector.quantize_mx(out=x_codes[:].bitcast(FP8X4), scales=x_scales[:], in_=grouped[:])
@@ -156,13 +160,13 @@ def rotate_and_store(nc, small, stage, js, rot, out_pjc):
     count = js.stop - js.start
     x = stage[:, js, 0:ROPE_CH]
     products = small.tile([P, 2, count, PAIRS, 2], F32)
-    nc.vector.tensor_tensor(
+    nc.gpsimd.tensor_tensor(
         out=products[:].rearrange("p o j i e -> p o j (i e)"),
         in0=x.unsqueeze(1).to_broadcast([P, 2, count, ROPE_CH]),
         in1=rot[:, :, js, :, :].rearrange("p o j i e -> p o j (i e)"),
         op=ALU.mult,
     )
-    nc.vector.tensor_tensor(
+    nc.gpsimd.tensor_tensor(
         out=x.rearrange("p j (i o) -> p o j i", o=2),
         in0=products[:, :, :, :, 0],
         in1=products[:, :, :, :, 1],
@@ -171,11 +175,13 @@ def rotate_and_store(nc, small, stage, js, rot, out_pjc):
     nc.sync.dma_start(out=out_pjc[:, js, :], in_=stage[:, js, :])
 
 
-def project(nc, stage_pool, small, psum_acc, x_mx, w_tiles, rot, out_pjc, per_store):
+def project(nc, stage_pool, small, psum_acc, x_mx, w_tiles, rot, out_pjc, per_store, midway=None):
     stage = stage_pool.tile([P, TOK_STORE, CH], F32)
     for first in range(0, TOK_STORE, per_store):
         for j in range(first, first + per_store):
             multiply(nc, psum_acc, stage, j, x_mx, w_tiles, (True, False))
+            if midway is not None and j == TOK_STORE // 2 - 1:
+                midway()
         rotate_and_store(nc, small, stage, slice(first, first + per_store), rot, out_pjc)
 
 
@@ -218,33 +224,34 @@ def tile_wqkv_pa_t_kernel(tc, Q_in, W_Q, W_K, out_0, out_1):
         halves = [slice(n * N_TILE, (n + 1) * N_TILE) for n in range(N_TILES)]
         quarters = [slice(u * CH // 4, (u + 1) * CH // 4) for u in range(4)]
 
-        x_mx = quantise_tokens(nc, staging, packed, transpose_tokens(nc, psum_t, identity, group_rows[0]))
+        grouped = copy_tokens(nc, staging, transpose_tokens(nc, psum_t, identity, group_rows[0]))
         wq = weight_tiles(weights, "q")
         interleave_weight(nc, True, raw_q, wq, halves[0])
+        x_ready = [quantise_tokens(nc, packed, grouped)]
         interleave_weight(nc, False, raw_q, wq, halves[1])
         quantise_weight(nc, wq, halves[0])
         quantise_weight(nc, wq, halves[1])
-
         wk = weight_tiles(weights, "k")
-        stage = stage_pool.tile([P, TOK_STORE, CH], F32)
-        interleave_weight(nc, True, raw_k, wk, quarters[0])
-        for j in range(TOK_STORE):
-            multiply(nc, psum_acc, stage, j, x_mx, wq, (False, False))
-            if j + 1 < 4:
-                interleave_weight(nc, True, raw_k, wk, quarters[j + 1])
+
+        for g in range(groups):
+            x_mx = x_ready[g]
+            if g == 0:
+                stage = stage_pool.tile([P, TOK_STORE, CH], F32)
+                interleave_weight(nc, True, raw_k, wk, quarters[0])
+                for j in range(TOK_STORE):
+                    multiply(nc, psum_acc, stage, j, x_mx, wq, (False, False))
+                    if j + 1 < 4:
+                        interleave_weight(nc, True, raw_k, wk, quarters[j + 1])
+                    else:
+                        quantise_weight(nc, wk, halves[0])
+                    rotate_and_store(nc, small, stage, slice(j, j + 1), group_rot[0], group_q[0])
+                quantise_weight(nc, wk, halves[1])
             else:
-                quantise_weight(nc, wk, halves[0])
-            rotate_and_store(nc, small, stage, slice(j, j + 1), group_rot[0], group_q[0])
-        quantise_weight(nc, wk, halves[1])
-
-        x_next = quantise_tokens(nc, staging, packed, transpose_tokens(nc, psum_t, identity, group_rows[1]))
-        project(nc, stage_pool, small, psum_acc, x_mx, wk, group_rot[0], group_k[0], 1)
-
-        for g in range(1, groups):
-            x_mx = x_next
+                project(nc, stage_pool, small, psum_acc, x_mx, wq, group_rot[g], group_q[g], TOK_STORE)
+            midway = None
             if g + 1 < groups:
-                banks = transpose_tokens(nc, psum_t, identity, group_rows[g + 1])
-            project(nc, stage_pool, small, psum_acc, x_mx, wq, group_rot[g], group_q[g], TOK_STORE)
-            if g + 1 < groups:
-                x_next = quantise_tokens(nc, staging, packed, banks)
-            project(nc, stage_pool, small, psum_acc, x_mx, wk, group_rot[g], group_k[g], TOK_STORE)
+                grouped = copy_tokens(nc, staging, transpose_tokens(nc, psum_t, identity, group_rows[g + 1]))
+                midway = lambda: x_ready.append(quantise_tokens(nc, packed, grouped))
+            project(
+                nc, stage_pool, small, psum_acc, x_mx, wk, group_rot[g], group_k[g], 1 if g == 0 else TOK_STORE, midway
+            )

@@ -24,6 +24,7 @@ TOK_STORE = 4
 STORES = TOK // TOK_STORE
 N_TILE = 512
 N_TILES = CH // N_TILE
+WHOLE_FROM = 2
 
 FLOPS = 2 * BATCH * SEQ * K * 2 * CH
 
@@ -75,10 +76,8 @@ def copy_on(nc, on_vector, out, in_):
         nc.scalar.copy(out=out, in_=in_)
 
 
-def load_weight(nc, weights, w, label):
-    raw = weights.tile([P, PACK, CH], BF16, name="raw_" + label)
+def load_weight(nc, raw, w):
     nc.sync.dma_start(out=raw[:], in_=w.rearrange("(p t) c -> p t c", t=PACK))
-    return raw
 
 
 def weight_tiles(weights, label):
@@ -119,25 +118,24 @@ def transpose_tokens(nc, psum_t, identity, rows):
     return banks
 
 
-def copy_tokens(nc, staging, banks):
-    grouped = staging.tile([P, TOK_STORE * P * PACK], BF16, align_bytes=64)
+def copy_tokens(nc, grouped, banks, m):
     grouped_words = grouped[:].bitcast(F32).rearrange("p (j r u) -> p j r u", j=TOK_STORE, u=2)
-    for m in range(TOK_STORE // 2):
-        nc.scalar.copy(
-            out=grouped_words[:, 2 * m : 2 * m + 2, :, :],
-            in_=banks[m][:].rearrange("p j u r -> p j r u"),
-        )
-    return grouped
+    nc.scalar.copy(
+        out=grouped_words[:, 2 * m : 2 * m + 2, :, :],
+        in_=banks[m][:].rearrange("p j u r -> p j r u"),
+    )
 
 
-def quantise_tokens(nc, packed, grouped):
-    x_codes = packed.tile([P, TOK_STORE * P], U32, align_bytes=64)
-    x_scales = packed.tile([P, TOK_STORE * P], U8, align_bytes=64)
-    nc.vector.quantize_mx(out=x_codes[:].bitcast(FP8X4), scales=x_scales[:], in_=grouped[:])
-    return x_codes, x_scales
+def quantise_tokens(nc, x_mx, grouped, toks):
+    x_codes, x_scales = x_mx
+    nc.vector.quantize_mx(
+        out=x_codes[:, toks].bitcast(FP8X4),
+        scales=x_scales[:, toks],
+        in_=grouped[:, PACK * toks.start : PACK * toks.stop],
+    )
 
 
-def multiply(nc, psum_acc, stage, j, x_mx, w_tiles, on_vector):
+def multiply(nc, psum_acc, stage, slot, x_mx, j, w_tiles, on_vector):
     x_codes, x_scales = x_mx
     w_codes, w_scales = w_tiles[1], w_tiles[2]
     toks = slice(j * P, (j + 1) * P)
@@ -153,7 +151,7 @@ def multiply(nc, psum_acc, stage, j, x_mx, w_tiles, on_vector):
             start=True,
             stop=True,
         )
-        copy_on(nc, on_vector[n], out=stage[:, j, cols], in_=acc[:])
+        copy_on(nc, on_vector[n], out=stage[:, slot, cols], in_=acc[:])
 
 
 def rotate_and_store(nc, small, stage, js, rot, out_pjc):
@@ -175,14 +173,24 @@ def rotate_and_store(nc, small, stage, js, rot, out_pjc):
     nc.sync.dma_start(out=out_pjc[:, js, :], in_=stage[:, js, :])
 
 
-def project(nc, stage_pool, small, psum_acc, x_mx, w_tiles, rot, out_pjc, per_store, midway=None):
-    stage = stage_pool.tile([P, TOK_STORE, CH], F32)
-    for first in range(0, TOK_STORE, per_store):
-        for j in range(first, first + per_store):
-            multiply(nc, psum_acc, stage, j, x_mx, w_tiles, (True, False))
-            if midway is not None and j == TOK_STORE // 2 - 1:
-                midway()
-        rotate_and_store(nc, small, stage, slice(first, first + per_store), rot, out_pjc)
+def project(nc, small, psum_acc, stage, first, x_mx, w_tiles, rot, out_pjc, stores, midway=None):
+    for j in range(TOK_STORE):
+        multiply(nc, psum_acc, stage, first + j, x_mx, j, w_tiles, (True, False))
+        if midway is not None and j == TOK_STORE // 2 - 1:
+            midway()
+        if j in stores:
+            rotate_and_store(nc, small, stage, stores[j], rot, out_pjc)
+
+
+def store_plan(g):
+    first = TOK_STORE * (g % STORES)
+    if g == 0:
+        return dict((j, slice(j, j + 1)) for j in range(TOK_STORE))
+    if g // STORES < WHOLE_FROM:
+        return {TOK_STORE - 1: slice(first, first + TOK_STORE)}
+    if g % STORES == STORES - 1:
+        return {TOK_STORE - 1: slice(0, TOK)}
+    return {}
 
 
 def tile_wqkv_pa_t_kernel(tc, Q_in, W_Q, W_K, out_0, out_1):
@@ -195,63 +203,95 @@ def tile_wqkv_pa_t_kernel(tc, Q_in, W_Q, W_K, out_0, out_1):
         packed = ctx.enter_context(tc.tile_pool(name="packed", bufs=2))
         staging = ctx.enter_context(tc.tile_pool(name="staging", bufs=2))
         small = ctx.enter_context(tc.tile_pool(name="small", bufs=2))
-        stage_pool = ctx.enter_context(tc.tile_pool(name="stage", bufs=8))
+        stage_pool = ctx.enter_context(tc.tile_pool(name="stage", bufs=4))
         psum_t = ctx.enter_context(tc.psum_pool(name="psum_t", bufs=2))
         psum_acc = ctx.enter_context(tc.psum_pool(name="psum_acc", bufs=6))
 
-        rows = [tokens.tile([P, TOK, K], BF16, name="rows%d" % b) for b in range(BATCH)]
-        group_rows, group_in, group_q, group_k, group_rot = [], [], [], [], []
+        rows = tokens.tile([P, BATCH, TOK, K], BF16)
+        rows_in = Q_in.rearrange("b (p j) k -> p b j k", j=TOK)
         rot = build_rotations(nc, consts)
+        group_rows = []
         for b in range(BATCH):
             for first in range(0, TOK, TOK_STORE):
-                js = slice(first, first + TOK_STORE)
-                group_rows.append(rows[b][:, js, :])
-                group_in.append(Q_in[b].rearrange("(p j) k -> p j k", j=TOK)[:, js, :])
-                group_q.append(out_0[b].rearrange("(p j) c -> p j c", j=TOK)[:, js, :])
-                group_k.append(out_1[b].rearrange("(p j) c -> p j c", j=TOK)[:, js, :])
-                group_rot.append(rot[:, :, js, :, :])
+                group_rows.append(rows[:, b, first : first + TOK_STORE, :])
         groups = len(group_rows)
+        out_q = [out_0[b].rearrange("(p j) c -> p j c", j=TOK) for b in range(BATCH)]
+        out_k = [out_1[b].rearrange("(p j) c -> p j c", j=TOK) for b in range(BATCH)]
 
-        nc.sync.dma_start(out=group_rows[0], in_=group_in[0])
-        raw_q = load_weight(nc, weights, W_Q, "q")
-        raw_k = load_weight(nc, weights, W_K, "k")
-        for g in range(1, groups):
-            nc.sync.dma_start(out=group_rows[g], in_=group_in[g])
+        halves = [slice(n * N_TILE, (n + 1) * N_TILE) for n in range(N_TILES)]
+        quarters = [slice(u * CH // 4, (u + 1) * CH // 4) for u in range(4)]
+        all_tokens = slice(0, TOK_STORE * P)
+
+        raw_q = weights.tile([P, PACK, CH], BF16, name="raw_q")
+        raw_k = weights.tile([P, PACK, CH], BF16, name="raw_k")
+        nc.sync.dma_start(out=rows[:, 0, 0:4, :], in_=rows_in[:, 0, 0:4, :])
+        load_weight(nc, raw_q, W_Q)
+        load_weight(nc, raw_k, W_K)
+        nc.sync.dma_start(out=rows[:, 0, 4:8, :], in_=rows_in[:, 0, 4:8, :])
+        nc.sync.dma_start(out=rows[:, 1, :, :], in_=rows_in[:, 1, :, :])
+        nc.sync.dma_start(
+            out=rows[:, 2:4, :, :].rearrange("p b j k -> p b (j k)"),
+            in_=rows_in[:, 2:4, :, :].rearrange("p b j k -> p b (j k)"),
+        )
 
         identity = consts.tile([P, P], F32)
         make_identity(nc, identity[:])
 
-        halves = [slice(n * N_TILE, (n + 1) * N_TILE) for n in range(N_TILES)]
-        quarters = [slice(u * CH // 4, (u + 1) * CH // 4) for u in range(4)]
+        def new_grouped():
+            grouped = staging.tile([P, TOK_STORE * P * PACK], BF16, align_bytes=64)
+            return grouped
 
-        grouped = copy_tokens(nc, staging, transpose_tokens(nc, psum_t, identity, group_rows[0]))
+        def new_packed():
+            x_codes = packed.tile([P, TOK_STORE * P], U32, align_bytes=64)
+            x_scales = packed.tile([P, TOK_STORE * P], U8, align_bytes=64)
+            return x_codes, x_scales
+
         wq = weight_tiles(weights, "q")
+        wk = weight_tiles(weights, "k")
+
+        banks = transpose_tokens(nc, psum_t, identity, group_rows[0])
+        grouped = new_grouped()
+        x_ready = [new_packed()]
+        copy_tokens(nc, grouped, banks, 0)
+        copy_tokens(nc, grouped, banks, 1)
         interleave_weight(nc, True, raw_q, wq, halves[0])
-        x_ready = [quantise_tokens(nc, packed, grouped)]
+        quantise_tokens(nc, x_ready[0], grouped, all_tokens)
         interleave_weight(nc, False, raw_q, wq, halves[1])
         quantise_weight(nc, wq, halves[0])
         quantise_weight(nc, wq, halves[1])
-        wk = weight_tiles(weights, "k")
+
+        def quantise_next(grouped_next):
+            x_ready.append(new_packed())
+            quantise_tokens(nc, x_ready[-1], grouped_next, all_tokens)
+
+        def new_stage():
+            stage = stage_pool.tile([P, TOK, CH], F32)
+            return stage
 
         for g in range(groups):
             x_mx = x_ready[g]
+            b = g // STORES
+            first = TOK_STORE * (g % STORES)
+            if first == 0:
+                stage_q = new_stage()
+                stage_k = new_stage()
             if g == 0:
-                stage = stage_pool.tile([P, TOK_STORE, CH], F32)
                 interleave_weight(nc, True, raw_k, wk, quarters[0])
                 for j in range(TOK_STORE):
-                    multiply(nc, psum_acc, stage, j, x_mx, wq, (False, False))
+                    multiply(nc, psum_acc, stage_q, j, x_mx, j, wq, (False, False))
                     if j + 1 < 4:
                         interleave_weight(nc, True, raw_k, wk, quarters[j + 1])
                     else:
                         quantise_weight(nc, wk, halves[0])
-                    rotate_and_store(nc, small, stage, slice(j, j + 1), group_rot[0], group_q[0])
+                    rotate_and_store(nc, small, stage_q, slice(j, j + 1), rot, out_q[0])
                 quantise_weight(nc, wk, halves[1])
             else:
-                project(nc, stage_pool, small, psum_acc, x_mx, wq, group_rot[g], group_q[g], TOK_STORE)
+                project(nc, small, psum_acc, stage_q, first, x_mx, wq, rot, out_q[b], store_plan(g))
             midway = None
             if g + 1 < groups:
-                grouped = copy_tokens(nc, staging, transpose_tokens(nc, psum_t, identity, group_rows[g + 1]))
-                midway = lambda: x_ready.append(quantise_tokens(nc, packed, grouped))
-            project(
-                nc, stage_pool, small, psum_acc, x_mx, wk, group_rot[g], group_k[g], 1 if g == 0 else TOK_STORE, midway
-            )
+                banks = transpose_tokens(nc, psum_t, identity, group_rows[g + 1])
+                grouped = new_grouped()
+                copy_tokens(nc, grouped, banks, 0)
+                copy_tokens(nc, grouped, banks, 1)
+                midway = lambda: quantise_next(grouped)
+            project(nc, small, psum_acc, stage_k, first, x_mx, wk, rot, out_k[b], store_plan(g), midway)

@@ -207,7 +207,7 @@ def tile_wqkv_pa_t_kernel(tc, Q_in, W_Q, W_K, out_0, out_1):
         psum_t = ctx.enter_context(tc.psum_pool(name="psum_t", bufs=2))
         psum_acc = ctx.enter_context(tc.psum_pool(name="psum_acc", bufs=6))
 
-        rows = tokens.tile([P, BATCH, TOK, K], BF16)
+        rows = tokens.tile([P, BATCH, TOK, K], BF16, align_bytes=256)
         rows_in = Q_in.rearrange("b (p j) k -> p b j k", j=TOK)
         rot = build_rotations(nc, consts)
         group_rows = []
@@ -222,8 +222,8 @@ def tile_wqkv_pa_t_kernel(tc, Q_in, W_Q, W_K, out_0, out_1):
         quarters = [slice(u * CH // 4, (u + 1) * CH // 4) for u in range(4)]
         all_tokens = slice(0, TOK_STORE * P)
 
-        raw_q = weights.tile([P, PACK, CH], BF16, name="raw_q")
-        raw_k = weights.tile([P, PACK, CH], BF16, name="raw_k")
+        raw_q = weights.tile([P, PACK, CH], BF16, name="raw_q", align_bytes=256)
+        raw_k = weights.tile([P, PACK, CH], BF16, name="raw_k", align_bytes=256)
         nc.sync.dma_start(out=rows[:, 0, 0:4, :], in_=rows_in[:, 0, 0:4, :])
         load_weight(nc, raw_q, W_Q)
         load_weight(nc, raw_k, W_K)
@@ -265,7 +265,7 @@ def tile_wqkv_pa_t_kernel(tc, Q_in, W_Q, W_K, out_0, out_1):
             quantise_tokens(nc, x_ready[-1], grouped_next, all_tokens)
 
         def new_stage():
-            stage = stage_pool.tile([P, TOK, CH], F32)
+            stage = stage_pool.tile([P, TOK, CH], F32, align_bytes=256)
             return stage
 
         for g in range(groups):

@@ -207,7 +207,7 @@ def tile_wqkv_pa_t_kernel(tc, Q_in, W_Q, W_K, out_0, out_1):
         psum_t = ctx.enter_context(tc.psum_pool(name="psum_t", bufs=2))
         psum_acc = ctx.enter_context(tc.psum_pool(name="psum_acc", bufs=6))
 
-        rows = tokens.tile([P, BATCH, TOK, K], BF16, align_bytes=256)
+        rows = tokens.tile([P, BATCH, TOK, K], BF16, align_bytes=4096)
         rows_in = Q_in.rearrange("b (p j) k -> p b j k", j=TOK)
         rot = build_rotations(nc, consts)
         group_rows = []
@@ -222,8 +222,8 @@ def tile_wqkv_pa_t_kernel(tc, Q_in, W_Q, W_K, out_0, out_1):
         quarters = [slice(u * CH // 4, (u + 1) * CH // 4) for u in range(4)]
         all_tokens = slice(0, TOK_STORE * P)
 
-        raw_q = weights.tile([P, PACK, CH], BF16, name="raw_q", align_bytes=256)
-        raw_k = weights.tile([P, PACK, CH], BF16, name="raw_k", align_bytes=256)
+        raw_q = weights.tile([P, PACK, CH], BF16, name="raw_q", align_bytes=4096)
+        raw_k = weights.tile([P, PACK, CH], BF16, name="raw_k", align_bytes=4096)
         nc.sync.dma_start(out=rows[:, 0, 0:4, :], in_=rows_in[:, 0, 0:4, :])
         load_weight(nc, raw_q, W_Q)
         load_weight(nc, raw_k, W_K)
@@ -265,7 +265,7 @@ def tile_wqkv_pa_t_kernel(tc, Q_in, W_Q, W_K, out_0, out_1):
             quantise_tokens(nc, x_ready[-1], grouped_next, all_tokens)
 
         def new_stage():
-            stage = stage_pool.tile([P, TOK, CH], F32, align_bytes=256)
+            stage = stage_pool.tile([P, TOK, CH], F32, align_bytes=4096)
             return stage
 
         for g in range(groups):

@@ -20,11 +20,10 @@ ROPE_CH = 16
 PAIRS = ROPE_CH // 2
 ROPE_BASE = 1e4
 TOK = SEQ // P
-TOK_STORE = 4
-STORES = TOK // TOK_STORE
+TILES = BATCH * TOK
+GROUP = 4
 N_TILE = 512
 N_TILES = CH // N_TILE
-WHOLE_FROM = 2
 
 FLOPS = 2 * BATCH * SEQ * K * 2 * CH
 
@@ -80,15 +79,7 @@ def load_weight(nc, raw, w):
     nc.sync.dma_start(out=raw[:], in_=w.rearrange("(p t) c -> p t c", t=PACK))
 
 
-def weight_tiles(weights, label):
-    grouped = weights.tile([P, CH, PACK], BF16, name="grouped_" + label, align_bytes=64)
-    codes = weights.tile([P, CH], U32, name="codes_" + label, align_bytes=64)
-    scales = weights.tile([P, CH], U8, name="scales_" + label, align_bytes=64)
-    return grouped, codes, scales
-
-
-def interleave_weight(nc, on_vector, raw, tiles, cols):
-    grouped = tiles[0]
+def interleave_weight(nc, on_vector, raw, grouped, cols):
     copy_on(
         nc,
         on_vector,
@@ -97,8 +88,8 @@ def interleave_weight(nc, on_vector, raw, tiles, cols):
     )
 
 
-def quantise_weight(nc, tiles, cols):
-    grouped, codes, scales = tiles
+def quantise_weight(nc, grouped, w_mx, cols):
+    codes, scales = w_mx
     nc.vector.quantize_mx(
         out=codes[:, cols].bitcast(FP8X4),
         scales=scales[:, cols],
@@ -108,7 +99,7 @@ def quantise_weight(nc, tiles, cols):
 
 def transpose_tokens(nc, psum_t, identity, rows):
     banks = []
-    for m in range(TOK_STORE // 2):
+    for m in range(GROUP // 2):
         flipped = psum_t.tile([P, 2, 2, P], F32)
         for jj in range(2):
             words = rows[:, 2 * m + jj, :].bitcast(F32).rearrange("r (q u) -> r u q", u=2)
@@ -119,25 +110,21 @@ def transpose_tokens(nc, psum_t, identity, rows):
 
 
 def copy_tokens(nc, grouped, banks, m):
-    grouped_words = grouped[:].bitcast(F32).rearrange("p (j r u) -> p j r u", j=TOK_STORE, u=2)
+    grouped_words = grouped[:].bitcast(F32).rearrange("p (j r u) -> p j r u", j=GROUP, u=2)
     nc.scalar.copy(
         out=grouped_words[:, 2 * m : 2 * m + 2, :, :],
         in_=banks[m][:].rearrange("p j u r -> p j r u"),
     )
 
 
-def quantise_tokens(nc, x_mx, grouped, toks):
+def quantise_tokens(nc, x_mx, grouped):
     x_codes, x_scales = x_mx
-    nc.vector.quantize_mx(
-        out=x_codes[:, toks].bitcast(FP8X4),
-        scales=x_scales[:, toks],
-        in_=grouped[:, PACK * toks.start : PACK * toks.stop],
-    )
+    nc.vector.quantize_mx(out=x_codes[:].bitcast(FP8X4), scales=x_scales[:], in_=grouped[:])
 
 
-def multiply(nc, psum_acc, stage, slot, x_mx, j, w_tiles, on_vector):
+def multiply(nc, psum_acc, stage, slot, x_mx, j, w_mx, on_vector):
     x_codes, x_scales = x_mx
-    w_codes, w_scales = w_tiles[1], w_tiles[2]
+    w_codes, w_scales = w_mx
     toks = slice(j * P, (j + 1) * P)
     for n in range(N_TILES):
         cols = slice(n * N_TILE, (n + 1) * N_TILE)
@@ -154,9 +141,10 @@ def multiply(nc, psum_acc, stage, slot, x_mx, j, w_tiles, on_vector):
         copy_on(nc, on_vector[n], out=stage[:, slot, cols], in_=acc[:])
 
 
-def rotate_and_store(nc, small, stage, js, rot, out_pjc):
-    count = js.stop - js.start
-    x = stage[:, js, 0:ROPE_CH]
+def rotate(nc, small, stage, slot, rot, j, count):
+    slots = slice(slot, slot + count)
+    js = slice(j, j + count)
+    x = stage[:, slots, 0:ROPE_CH]
     products = small.tile([P, 2, count, PAIRS, 2], F32)
     nc.gpsimd.tensor_tensor(
         out=products[:].rearrange("p o j i e -> p o j (i e)"),
@@ -170,128 +158,141 @@ def rotate_and_store(nc, small, stage, js, rot, out_pjc):
         in1=products[:, :, :, :, 1],
         op=ALU.add,
     )
-    nc.sync.dma_start(out=out_pjc[:, js, :], in_=stage[:, js, :])
 
 
-def project(nc, small, psum_acc, stage, first, x_mx, w_tiles, rot, out_pjc, stores, midway=None):
-    for j in range(TOK_STORE):
-        multiply(nc, psum_acc, stage, first + j, x_mx, j, w_tiles, (True, False))
-        if midway is not None and j == TOK_STORE // 2 - 1:
-            midway()
-        if j in stores:
-            rotate_and_store(nc, small, stage, stores[j], rot, out_pjc)
+def store(nc, out, first, count, tiles):
+    b, j = divmod(first, TOK)
+    if count <= TOK:
+        nc.sync.dma_start(out=out[:, b, j : j + count, :], in_=tiles)
+    else:
+        nc.sync.dma_start(
+            out=out[:, b : b + count // TOK, :, :].rearrange("p b j c -> p b (j c)"),
+            in_=tiles.rearrange("p (b j) c -> p b (j c)", j=TOK),
+        )
 
 
-def store_plan(g):
-    first = TOK_STORE * (g % STORES)
-    if g == 0:
-        return dict((j, slice(j, j + 1)) for j in range(TOK_STORE))
-    if g // STORES < WHOLE_FROM:
-        return {TOK_STORE - 1: slice(first, first + TOK_STORE)}
-    if g % STORES == STORES - 1:
-        return {TOK_STORE - 1: slice(0, TOK)}
-    return {}
+RUNS = (
+    ("q", 0, 2), ("q", 2, 2), ("k", 0, 2), ("k", 2, 2), ("q", 4, 4), ("k", 4, 4),
+    ("q", 8, 8), ("k", 8, 8),
+    ("q", 16, 8), ("k", 16, 16), ("q", 24, 8),
+)
+SLOTS = 32
+
+
+def token_plan():
+    fetch = {}
+    quantise = {}
+    seen = {0}
+    made = 0
+    for label, first, count in RUNS:
+        for j in range(first, first + count):
+            g = j // GROUP
+            if g not in seen:
+                seen.add(g)
+                fetch[made - GROUP] = g
+                quantise[made - GROUP // 2] = g
+            made += 1
+    return fetch, quantise
+
+
+FETCH, QUANTISE = token_plan()
 
 
 def tile_wqkv_pa_t_kernel(tc, Q_in, W_Q, W_K, out_0, out_1):
     nc = tc.nc
     with ExitStack() as ctx:
         ctx.enter_context(tc.manual_schedule())
-        consts = ctx.enter_context(tc.tile_pool(name="consts", bufs=1))
+        moved = ctx.enter_context(tc.tile_pool(name="moved", bufs=1))
         weights = ctx.enter_context(tc.tile_pool(name="weights", bufs=1))
-        tokens = ctx.enter_context(tc.tile_pool(name="tokens", bufs=1))
-        packed = ctx.enter_context(tc.tile_pool(name="packed", bufs=2))
+        packed = ctx.enter_context(tc.tile_pool(name="packed", bufs=5))
         staging = ctx.enter_context(tc.tile_pool(name="staging", bufs=2))
+        consts = ctx.enter_context(tc.tile_pool(name="consts", bufs=1))
         small = ctx.enter_context(tc.tile_pool(name="small", bufs=2))
-        stage_pool = ctx.enter_context(tc.tile_pool(name="stage", bufs=4))
         psum_t = ctx.enter_context(tc.psum_pool(name="psum_t", bufs=2))
         psum_acc = ctx.enter_context(tc.psum_pool(name="psum_acc", bufs=6))
 
-        rows = tokens.tile([P, BATCH, TOK, K], BF16, align_bytes=4096)
+        rows = moved.tile([P, BATCH, TOK, K], BF16, align_bytes=4096)
+        tile_rows = rows[:].rearrange("p b j k -> p (b j) k")
+        raw_q = moved.tile([P, PACK, CH], BF16, name="raw_q", align_bytes=4096)
+        raw_k = moved.tile([P, PACK, CH], BF16, name="raw_k", align_bytes=4096)
+        stage = moved.tile([P, SLOTS, CH], F32, align_bytes=4096)
         rows_in = Q_in.rearrange("b (p j) k -> p b j k", j=TOK)
+        out_of = {
+            "q": out_0.rearrange("b (p j) c -> p b j c", j=TOK),
+            "k": out_1.rearrange("b (p j) c -> p b j c", j=TOK),
+        }
         rot = build_rotations(nc, consts)
-        group_rows = []
-        for b in range(BATCH):
-            for first in range(0, TOK, TOK_STORE):
-                group_rows.append(rows[:, b, first : first + TOK_STORE, :])
-        groups = len(group_rows)
-        out_q = [out_0[b].rearrange("(p j) c -> p j c", j=TOK) for b in range(BATCH)]
-        out_k = [out_1[b].rearrange("(p j) c -> p j c", j=TOK) for b in range(BATCH)]
 
         halves = [slice(n * N_TILE, (n + 1) * N_TILE) for n in range(N_TILES)]
         quarters = [slice(u * CH // 4, (u + 1) * CH // 4) for u in range(4)]
-        all_tokens = slice(0, TOK_STORE * P)
 
-        raw_q = weights.tile([P, PACK, CH], BF16, name="raw_q", align_bytes=4096)
-        raw_k = weights.tile([P, PACK, CH], BF16, name="raw_k", align_bytes=4096)
         nc.sync.dma_start(out=rows[:, 0, 0:4, :], in_=rows_in[:, 0, 0:4, :])
         load_weight(nc, raw_q, W_Q)
         load_weight(nc, raw_k, W_K)
         nc.sync.dma_start(out=rows[:, 0, 4:8, :], in_=rows_in[:, 0, 4:8, :])
-        nc.sync.dma_start(out=rows[:, 1, :, :], in_=rows_in[:, 1, :, :])
         nc.sync.dma_start(
-            out=rows[:, 2:4, :, :].rearrange("p b j k -> p b (j k)"),
-            in_=rows_in[:, 2:4, :, :].rearrange("p b j k -> p b (j k)"),
+            out=rows[:, 1:BATCH, :, :].rearrange("p b j k -> p b (j k)"),
+            in_=rows_in[:, 1:BATCH, :, :].rearrange("p b j k -> p b (j k)"),
         )
 
         identity = consts.tile([P, P], F32)
         make_identity(nc, identity[:])
 
+        x_mx = []
+        w_mx = {}
+        for label in ("q", "k"):
+            codes = weights.tile([P, CH], U32, name="codes_" + label, align_bytes=64)
+            scales = weights.tile([P, CH], U8, name="scales_" + label, align_bytes=64)
+            w_mx[label] = (codes, scales)
+
         def new_grouped():
-            grouped = staging.tile([P, TOK_STORE * P * PACK], BF16, align_bytes=64)
+            grouped = staging.tile([P, GROUP * P * PACK], BF16, align_bytes=64)
             return grouped
 
-        def new_packed():
-            x_codes = packed.tile([P, TOK_STORE * P], U32, align_bytes=64)
-            x_scales = packed.tile([P, TOK_STORE * P], U8, align_bytes=64)
-            return x_codes, x_scales
+        def quantise_group(grouped):
+            x_codes = packed.tile([P, GROUP * P], U32, align_bytes=64)
+            x_scales = packed.tile([P, GROUP * P], U8, align_bytes=64)
+            x_mx.append((x_codes, x_scales))
+            quantise_tokens(nc, x_mx[-1], grouped)
 
-        wq = weight_tiles(weights, "q")
-        wk = weight_tiles(weights, "k")
+        def new_grouped_w():
+            grouped_w = weights.tile([P, CH, PACK], BF16, align_bytes=64)
+            return grouped_w
 
-        banks = transpose_tokens(nc, psum_t, identity, group_rows[0])
-        grouped = new_grouped()
-        x_ready = [new_packed()]
-        copy_tokens(nc, grouped, banks, 0)
-        copy_tokens(nc, grouped, banks, 1)
-        interleave_weight(nc, True, raw_q, wq, halves[0])
-        quantise_tokens(nc, x_ready[0], grouped, all_tokens)
-        interleave_weight(nc, False, raw_q, wq, halves[1])
-        quantise_weight(nc, wq, halves[0])
-        quantise_weight(nc, wq, halves[1])
+        def fetch_tokens(g):
+            banks = transpose_tokens(nc, psum_t, identity, tile_rows[:, g * GROUP : (g + 1) * GROUP, :])
+            grouped = new_grouped()
+            copy_tokens(nc, grouped, banks, 0)
+            copy_tokens(nc, grouped, banks, 1)
+            return grouped
 
-        def quantise_next(grouped_next):
-            x_ready.append(new_packed())
-            quantise_tokens(nc, x_ready[-1], grouped_next, all_tokens)
+        grouped = fetch_tokens(0)
+        grouped_q = new_grouped_w()
+        interleave_weight(nc, True, raw_q, grouped_q, halves[0])
+        quantise_group(grouped)
+        interleave_weight(nc, False, raw_q, grouped_q, halves[1])
+        quantise_weight(nc, grouped_q, w_mx["q"], halves[0])
+        quantise_weight(nc, grouped_q, w_mx["q"], halves[1])
+        grouped_k = new_grouped_w()
+        interleave_weight(nc, True, raw_k, grouped_k, quarters[0])
 
-        def new_stage():
-            stage = stage_pool.tile([P, TOK, CH], F32, align_bytes=4096)
-            return stage
-
-        for g in range(groups):
-            x_mx = x_ready[g]
-            b = g // STORES
-            first = TOK_STORE * (g % STORES)
-            if first == 0:
-                stage_q = new_stage()
-                stage_k = new_stage()
-            if g == 0:
-                interleave_weight(nc, True, raw_k, wk, quarters[0])
-                for j in range(TOK_STORE):
-                    multiply(nc, psum_acc, stage_q, j, x_mx, j, wq, (False, False))
-                    if j + 1 < 4:
-                        interleave_weight(nc, True, raw_k, wk, quarters[j + 1])
-                    else:
-                        quantise_weight(nc, wk, halves[0])
-                    rotate_and_store(nc, small, stage_q, slice(j, j + 1), rot, out_q[0])
-                quantise_weight(nc, wk, halves[1])
-            else:
-                project(nc, small, psum_acc, stage_q, first, x_mx, wq, rot, out_q[b], store_plan(g))
-            midway = None
-            if g + 1 < groups:
-                banks = transpose_tokens(nc, psum_t, identity, group_rows[g + 1])
-                grouped = new_grouped()
-                copy_tokens(nc, grouped, banks, 0)
-                copy_tokens(nc, grouped, banks, 1)
-                midway = lambda: quantise_next(grouped)
-            project(nc, small, psum_acc, stage_k, first, x_mx, wk, rot, out_k[b], store_plan(g), midway)
+        made = 0
+        for label, first, count in RUNS:
+            run_slot = made % SLOTS
+            for j in range(first, first + count):
+                if made in QUANTISE:
+                    quantise_group(grouped)
+                if made in FETCH:
+                    grouped = fetch_tokens(FETCH[made])
+                on_vector = (made >= GROUP - 1, False)
+                multiply(nc, psum_acc, stage, made % SLOTS, x_mx[j // GROUP], j % GROUP, w_mx[label], on_vector)
+                if made < GROUP - 1:
+                    interleave_weight(nc, True, raw_k, grouped_k, quarters[made + 1])
+                elif made == GROUP - 1:
+                    quantise_weight(nc, grouped_k, w_mx["k"], halves[0])
+                    quantise_weight(nc, grouped_k, w_mx["k"], halves[1])
+                made += 1
+                since = (j - first) % GROUP + 1
+                if since == GROUP or j == first + count - 1:
+                    rotate(nc, small, stage, (made - since) % SLOTS, rot, (j + 1 - since) % TOK, since)
+            store(nc, out_of[label], first, count, stage[:, run_slot : run_slot + count, :])

import math
from contextlib import ExitStack

import concourse.mybir as mybir
from concourse.masks import make_identity

F32 = mybir.dt.float32
BF16 = mybir.dt.bfloat16
I32 = mybir.dt.int32
U32 = mybir.dt.uint32
U8 = mybir.dt.uint8
FP8X4 = mybir.dt.float8_e4m3fn_x4
ALU = mybir.AluOpType
ACT = mybir.ActivationFunctionType

P = 128
PACK = 4
BATCH, SEQ, K, CH = 4, 1024, 512, 1024
ROPE_CH = 16
PAIRS = ROPE_CH // 2
ROPE_BASE = 1e4
TOK = SEQ // P
TILES = BATCH * TOK
GROUP = 4
N_TILE = 512
N_TILES = CH // N_TILE

FLOPS = 2 * BATCH * SEQ * K * 2 * CH

TWO_PI = 2.0 * math.pi
TURN_GRID = 2.0 ** 15
ROUND_MAGIC = 1.5 * 2.0 ** 23


def build_rotations(nc, consts):
    position_int = consts.tile([P, TOK], I32)
    nc.gpsimd.iota(position_int[:], pattern=[[1, TOK]], base=0, channel_multiplier=TOK)
    position = consts.tile([P, TOK], F32)
    nc.vector.tensor_copy(out=position[:], in_=position_int[:])

    coarse = consts.tile([P, 2, TOK, PAIRS], F32)
    fine = consts.tile([P, TOK, PAIRS], F32)
    for i in range(PAIRS):
        turns = ROPE_BASE ** (-2.0 * i / ROPE_CH) / TWO_PI
        turns_coarse = round(turns * TURN_GRID) / TURN_GRID
        nc.vector.tensor_scalar_mul(out=coarse[:, 0, :, i], in0=position[:], scalar1=turns_coarse)
        nc.vector.tensor_scalar_mul(out=fine[:, :, i], in0=position[:], scalar1=turns - turns_coarse)
    nc.vector.tensor_scalar_add(out=coarse[:, 1, :, :], in0=coarse[:, 0, :, :], scalar1=0.25)

    fine_twice = fine[:].unsqueeze(1).to_broadcast([P, 2, TOK, PAIRS])
    whole = consts.tile([P, 2, TOK, PAIRS], F32)
    nc.vector.tensor_tensor(out=whole[:], in0=coarse[:], in1=fine_twice, op=ALU.add)
    nc.vector.tensor_scalar(
        out=whole[:], in0=whole[:], scalar1=ROUND_MAGIC, scalar2=ROUND_MAGIC, op0=ALU.add, op1=ALU.subtract
    )
    nc.vector.tensor_tensor(out=coarse[:], in0=coarse[:], in1=whole[:], op=ALU.subtract)
    reduced = consts.tile([P, 2, TOK, PAIRS], F32)
    nc.vector.tensor_tensor(out=reduced[:], in0=coarse[:], in1=fine_twice, op=ALU.add)

    rot = consts.tile([P, 2, TOK, PAIRS, 2], F32)
    for o in range(2):
        for e in range(2):
            quarter_ahead = 1 if o == e else 0
            sign = -1.0 if o < e else 1.0
            nc.scalar.activation(
                out=rot[:, o, :, :, e], in_=reduced[:, quarter_ahead, :, :], func=ACT.Sin, scale=sign * TWO_PI
            )
    return rot


def copy_on(nc, on_vector, out, in_):
    if on_vector:
        nc.vector.tensor_copy(out=out, in_=in_)
    else:
        nc.scalar.copy(out=out, in_=in_)


def load_weight(nc, raw, w):
    nc.sync.dma_start(out=raw[:], in_=w.rearrange("(p t) c -> p t c", t=PACK))


def interleave_weight(nc, on_vector, raw, grouped, cols):
    copy_on(
        nc,
        on_vector,
        out=grouped[:, cols, :].rearrange("p (c i) t -> p c t i", i=4),
        in_=raw[:, :, cols].rearrange("p t (c i) -> p c t i", i=4),
    )


def quantise_weight(nc, grouped, w_mx, cols):
    codes, scales = w_mx
    nc.vector.quantize_mx(
        out=codes[:, cols].bitcast(FP8X4),
        scales=scales[:, cols],
        in_=grouped[:, cols, :].rearrange("p c t -> p (c t)"),
    )


def transpose_tokens(nc, psum_t, identity, rows):
    banks = []
    for m in range(GROUP // 2):
        flipped = psum_t.tile([P, 2, 2, P], F32)
        for jj in range(2):
            words = rows[:, 2 * m + jj, :].bitcast(F32).rearrange("r (q u) -> r u q", u=2)
            for u in range(2):
                nc.tensor.transpose(out=flipped[:, jj, u, :], in_=words[:, u, :], identity=identity[:])
        banks.append(flipped)
    return banks


def copy_tokens(nc, grouped, banks, m):
    grouped_words = grouped[:].bitcast(F32).rearrange("p (j r u) -> p j r u", j=GROUP, u=2)
    nc.scalar.copy(
        out=grouped_words[:, 2 * m : 2 * m + 2, :, :],
        in_=banks[m][:].rearrange("p j u r -> p j r u"),
    )


def quantise_tokens(nc, x_mx, grouped):
    x_codes, x_scales = x_mx
    nc.vector.quantize_mx(out=x_codes[:].bitcast(FP8X4), scales=x_scales[:], in_=grouped[:])


def multiply(nc, psum_acc, stage, slot, x_mx, j, w_mx, on_vector):
    x_codes, x_scales = x_mx
    w_codes, w_scales = w_mx
    toks = slice(j * P, (j + 1) * P)
    for n in range(N_TILES):
        cols = slice(n * N_TILE, (n + 1) * N_TILE)
        acc = psum_acc.tile([P, N_TILE], F32)
        nc.tensor.matmul_mx(
            out=acc[:],
            lhsT=x_codes[:, toks].bitcast(FP8X4),
            lhsT_scale=x_scales[:, toks],
            rhs=w_codes[:, cols].bitcast(FP8X4),
            rhs_scale=w_scales[:, cols],
            start=True,
            stop=True,
        )
        copy_on(nc, on_vector[n], out=stage[:, slot, cols], in_=acc[:])


def rotate(nc, small, stage, slot, rot, j, count):
    slots = slice(slot, slot + count)
    js = slice(j, j + count)
    x = stage[:, slots, 0:ROPE_CH]
    products = small.tile([P, 2, count, PAIRS, 2], F32)
    nc.gpsimd.tensor_tensor(
        out=products[:].rearrange("p o j i e -> p o j (i e)"),
        in0=x.unsqueeze(1).to_broadcast([P, 2, count, ROPE_CH]),
        in1=rot[:, :, js, :, :].rearrange("p o j i e -> p o j (i e)"),
        op=ALU.mult,
    )
    nc.gpsimd.tensor_tensor(
        out=x.rearrange("p j (i o) -> p o j i", o=2),
        in0=products[:, :, :, :, 0],
        in1=products[:, :, :, :, 1],
        op=ALU.add,
    )


def store(nc, out, first, count, tiles):
    b, j = divmod(first, TOK)
    if count <= TOK:
        nc.sync.dma_start(out=out[:, b, j : j + count, :], in_=tiles)
    else:
        nc.sync.dma_start(
            out=out[:, b : b + count // TOK, :, :].rearrange("p b j c -> p b (j c)"),
            in_=tiles.rearrange("p (b j) c -> p b (j c)", j=TOK),
        )


RUNS = (
    ("q", 0, 2), ("q", 2, 2), ("k", 0, 2), ("k", 2, 2), ("q", 4, 4), ("k", 4, 4),
    ("q", 8, 8), ("k", 8, 8),
    ("q", 16, 8), ("k", 16, 16), ("q", 24, 8),
)
SLOTS = 32


def token_plan():
    fetch = {}
    quantise = {}
    seen = {0}
    made = 0
    for label, first, count in RUNS:
        for j in range(first, first + count):
            g = j // GROUP
            if g not in seen:
                seen.add(g)
                fetch[made - GROUP] = g
                quantise[made - GROUP // 2] = g
            made += 1
    return fetch, quantise


FETCH, QUANTISE = token_plan()


def tile_wqkv_pa_t_kernel(tc, Q_in, W_Q, W_K, out_0, out_1):
    nc = tc.nc
    with ExitStack() as ctx:
        ctx.enter_context(tc.manual_schedule())
        moved = ctx.enter_context(tc.tile_pool(name="moved", bufs=1))
        weights = ctx.enter_context(tc.tile_pool(name="weights", bufs=1))
        packed = ctx.enter_context(tc.tile_pool(name="packed", bufs=5))
        staging = ctx.enter_context(tc.tile_pool(name="staging", bufs=2))
        consts = ctx.enter_context(tc.tile_pool(name="consts", bufs=1))
        small = ctx.enter_context(tc.tile_pool(name="small", bufs=2))
        psum_t = ctx.enter_context(tc.psum_pool(name="psum_t", bufs=2))
        psum_acc = ctx.enter_context(tc.psum_pool(name="psum_acc", bufs=6))

        rows = moved.tile([P, BATCH, TOK, K], BF16, align_bytes=4096)
        tile_rows = rows[:].rearrange("p b j k -> p (b j) k")
        raw_q = moved.tile([P, PACK, CH], BF16, name="raw_q", align_bytes=4096)
        raw_k = moved.tile([P, PACK, CH], BF16, name="raw_k", align_bytes=4096)
        stage = moved.tile([P, SLOTS, CH], F32, align_bytes=4096)
        rows_in = Q_in.rearrange("b (p j) k -> p b j k", j=TOK)
        out_of = {
            "q": out_0.rearrange("b (p j) c -> p b j c", j=TOK),
            "k": out_1.rearrange("b (p j) c -> p b j c", j=TOK),
        }
        rot = build_rotations(nc, consts)

        halves = [slice(n * N_TILE, (n + 1) * N_TILE) for n in range(N_TILES)]
        quarters = [slice(u * CH // 4, (u + 1) * CH // 4) for u in range(4)]

        nc.sync.dma_start(out=rows[:, 0, 0:4, :], in_=rows_in[:, 0, 0:4, :])
        load_weight(nc, raw_q, W_Q)
        load_weight(nc, raw_k, W_K)
        nc.sync.dma_start(out=rows[:, 0, 4:8, :], in_=rows_in[:, 0, 4:8, :])
        nc.sync.dma_start(
            out=rows[:, 1:BATCH, :, :].rearrange("p b j k -> p b (j k)"),
            in_=rows_in[:, 1:BATCH, :, :].rearrange("p b j k -> p b (j k)"),
        )

        identity = consts.tile([P, P], F32)
        make_identity(nc, identity[:])

        x_mx = []
        w_mx = {}
        for label in ("q", "k"):
            codes = weights.tile([P, CH], U32, name="codes_" + label, align_bytes=64)
            scales = weights.tile([P, CH], U8, name="scales_" + label, align_bytes=64)
            w_mx[label] = (codes, scales)

        def new_grouped():
            grouped = staging.tile([P, GROUP * P * PACK], BF16, align_bytes=64)
            return grouped

        def quantise_group(grouped):
            x_codes = packed.tile([P, GROUP * P], U32, align_bytes=64)
            x_scales = packed.tile([P, GROUP * P], U8, align_bytes=64)
            x_mx.append((x_codes, x_scales))
            quantise_tokens(nc, x_mx[-1], grouped)

        def new_grouped_w():
            grouped_w = weights.tile([P, CH, PACK], BF16, align_bytes=64)
            return grouped_w

        def fetch_tokens(g):
            banks = transpose_tokens(nc, psum_t, identity, tile_rows[:, g * GROUP : (g + 1) * GROUP, :])
            grouped = new_grouped()
            copy_tokens(nc, grouped, banks, 0)
            copy_tokens(nc, grouped, banks, 1)
            return grouped

        grouped = fetch_tokens(0)
        grouped_q = new_grouped_w()
        interleave_weight(nc, True, raw_q, grouped_q, halves[0])
        quantise_group(grouped)
        interleave_weight(nc, False, raw_q, grouped_q, halves[1])
        quantise_weight(nc, grouped_q, w_mx["q"], halves[0])
        quantise_weight(nc, grouped_q, w_mx["q"], halves[1])
        grouped_k = new_grouped_w()
        interleave_weight(nc, True, raw_k, grouped_k, quarters[0])

        made = 0
        for label, first, count in RUNS:
            run_slot = made % SLOTS
            for j in range(first, first + count):
                if made in QUANTISE:
                    quantise_group(grouped)
                if made in FETCH:
                    grouped = fetch_tokens(FETCH[made])
                on_vector = (made >= GROUP - 1, False)
                multiply(nc, psum_acc, stage, made % SLOTS, x_mx[j // GROUP], j % GROUP, w_mx[label], on_vector)
                if made < GROUP - 1:
                    interleave_weight(nc, True, raw_k, grouped_k, quarters[made + 1])
                elif made == GROUP - 1:
                    quantise_weight(nc, grouped_k, w_mx["k"], halves[0])
                    quantise_weight(nc, grouped_k, w_mx["k"], halves[1])
                made += 1
                since = (j - first) % GROUP + 1
                if since == GROUP or j == first + count - 1:
                    rotate(nc, small, stage, (made - since) % SLOTS, rot, (j + 1 - since) % TOK, since)
            store(nc, out_of[label], first, count, stage[:, run_slot : run_slot + count, :])
